import numpy as np
import ml_dtypes


def mxq(x, axis, fmt="e4m3"):
    dtype, down = {"e4m3": (ml_dtypes.float8_e4m3fn, 7), "e5m2": (ml_dtypes.float8_e5m2, 14)}[fmt]
    v = np.moveaxis(np.asarray(x, np.float32).astype(ml_dtypes.bfloat16).astype(np.float64), axis, -1)
    blocks = v.reshape(v.shape[:-1] + (-1, 32))
    amax = np.abs(blocks).max(-1, keepdims=True)
    byte = np.maximum(np.where(amax > 0, np.frexp(amax)[1] - 1 + 127, 0) - down, 1)
    scale = np.exp2(byte - 127.0)
    codes = (blocks / scale).astype(np.float32).astype(dtype).astype(np.float64)
    return np.moveaxis((codes * scale).reshape(v.shape), -1, axis)


WIDE = False


def mx_kscale(k):
    if not WIDE:
        return np.ones(k)
    levels = np.array([10, -10, 5, -5, 0])
    if k % 512:
        return np.exp2(np.random.permutation(np.resize(levels, k // 32))).repeat(32)
    a = np.empty((k // 512, 16))
    for p in range(k // 512):
        a[p, :8] = np.random.permutation(np.resize(levels, 8))
        for g in range(8):
            far = levels[np.abs(levels - a[p, g]) >= 10]
            a[p, g + 8] = far[np.random.randint(len(far))]
    return np.exp2(a.ravel()).repeat(32)


BF16 = ml_dtypes.bfloat16


def bf(x):
    return np.asarray(x, np.float32).astype(BF16)


def f64(x):
    return np.asarray(x).astype(np.float64)


B, L, E, H = 4, 64, 2048, 16
HD = E // H
EPS = 1e-12


def l2_normalize(t):
    n = np.sqrt(np.sum(t * t, axis=-1, keepdims=True))
    return t / np.maximum(n, EPS)


def setup_inputs():
    s = mx_kscale(E)
    return {"x": bf(np.random.standard_normal((B, L, E)) * s),
            "W": bf(np.random.standard_normal((3 * E, E)) / np.sqrt(E) / s[None, :]),
            "b": bf(np.random.standard_normal(3 * E) * 0.3)}


def reference(x, W, b):
    y = (mxq(f64(x), 2, "e4m3") @ mxq(f64(W), 1, "e4m3").T) + f64(b)
    y = y.reshape(B, L, H, 3, HD)
    q = np.transpose(y[..., 0, :], (0, 2, 1, 3))
    k = np.transpose(y[..., 1, :], (0, 2, 1, 3))
    v = np.transpose(y[..., 2, :], (0, 2, 1, 3))
    return l2_normalize(q), l2_normalize(k), v

@@ -1,0 +1,283 @@
+from contextlib import ExitStack
+
+import concourse.mybir as mybir
+from concourse.masks import make_identity
+
+F32 = mybir.dt.float32
+BF16 = mybir.dt.bfloat16
+U32 = mybir.dt.uint32
+U8 = mybir.dt.uint8
+I32 = mybir.dt.int32
+FP8X4 = mybir.dt.float8_e4m3fn_x4
+ALU = mybir.AluOpType
+ACT = mybir.ActivationFunctionType
+
+P = 128
+E = 2048
+NH = 16
+HD = 128
+NBLK = 12
+NSLOT = 2 * NBLK
+W_AHEAD = 12
+T_BANKS = 5
+FLOPS = 2 * 256 * 2048 * 6144
+
+
+def tile_selfattention_pa_kernel(tc, x, W, b, out_0, out_1, out_2):
+    nc = tc.nc
+    outs = (out_0, out_1, out_2)
+    with ExitStack() as ctx:
+        const = ctx.enter_context(tc.tile_pool(name="const", bufs=1))
+        wpool = ctx.enter_context(tc.tile_pool(name="wpool", bufs=W_AHEAD))
+        gpool = ctx.enter_context(tc.tile_pool(name="gpool", bufs=8))
+        cpool = ctx.enter_context(tc.tile_pool(name="cpool", bufs=6))
+        ypool = ctx.enter_context(tc.tile_pool(name="ypool", bufs=6))
+        spool = ctx.enter_context(tc.tile_pool(name="spool", bufs=4))
+        tpsum = ctx.enter_context(tc.psum_pool(name="tpsum", bufs=T_BANKS))
+        opsum = ctx.enter_context(tc.psum_pool(name="opsum", bufs=8 - T_BANKS))
+        ctx.enter_context(tc.manual_schedule())
+
+        ident_f = const.tile([P, P], F32, name="ident_f")
+        ident_b = const.tile([P, P], BF16, name="ident_b")
+        b_sb = const.tile([P, 384], BF16, name="b_sb")
+        bias_bc = const.tile([P, 6144], BF16, name="bias_bc")
+        warm = const.tile([P, 1], F32, name="warm")
+        warm2 = const.tile([P, 1], F32, name="warm2")
+        x_sb = [const.tile([P, E], BF16, name="x_sb%d" % m) for m in range(2)]
+        xg = const.tile([P, 4096], BF16, name="xg", align_bytes=64)
+        xc = const.tile([P, 1024], U32, name="xc", align_bytes=64)
+        xs = const.tile([P, 1024], U8, name="xs", align_bytes=64)
+
+        w_tiles = {}
+
+        def load_w(k):
+            blk = k // 2
+            tt = k % 2
+            rows = W[512 * blk:512 * (blk + 1), :].rearrange("(p t) k -> p t k", t=4)
+            w_sb = wpool.tile([P, 2, E], BF16, name="w_sb")
+            nc.sync.dma_start(out=w_sb[:], in_=rows[:, 2 * tt:2 * tt + 2, :])
+            w_tiles[k] = w_sb
+
+        nc.vector.memset(b_sb[:].bitcast(I32), 0)
+        nc.vector.memset(warm[:], 1.0)
+        nc.sync.dma_start(out=b_sb[0:16, :], in_=b.rearrange("(h n) -> h n", h=16))
+        for m in range(2):
+            for bl in range(2):
+                nc.sync.dma_start(out=x_sb[m][bl:P:2, :], in_=x[2 * m + bl, :, :])
+        for k in range(W_AHEAD):
+            load_w(k)
+        make_identity(nc, ident_b[:])
+        make_identity(nc, ident_f[:])
+        nc.scalar.sqrt(out=warm2[:], in_=warm[:])
+
+        def drain(on_vector, dst, src):
+            if on_vector:
+                nc.vector.tensor_copy(out=dst, in_=src)
+            else:
+                nc.scalar.copy(out=dst, in_=src)
+
+        for h in range(NH):
+            tb = tpsum.tile([P, 512], F32, name="tb")
+            nc.tensor.matmul(
+                out=tb[:, 0:384],
+                lhsT=ident_b[:, h:h + 1].to_broadcast([P, P]),
+                rhs=b_sb[:],
+                start=True,
+                stop=True,
+            )
+            drain(h % 2 == 0, bias_bc[:, 384 * h:384 * (h + 1)], tb[:, 0:384])
+
+        def transposes_into_bank(src32, col0, step_a):
+            tb = tpsum.tile([P, 512], F32, name="tb")
+            for a in range(2):
+                for u in range(2):
+                    c0 = col0 + a * step_a + u
+                    nc.tensor.transpose(
+                        out=tb[:, (2 * a + u) * P:(2 * a + u + 1) * P],
+                        in_=src32[:, c0:c0 + 2 * P - 1:2],
+                        identity=ident_f[:],
+                    )
+            return tb
+
+        def drain_bank(on_vector, dst32, tb):
+            drain(
+                on_vector,
+                dst32.rearrange("q (a c u) -> q a c u", a=2, u=2),
+                tb[:].rearrange("q (a u c) -> q a c u", a=2, u=2),
+            )
+
+        xg32 = xg[:].bitcast(F32)
+        for m in range(2):
+            x32 = x_sb[m][:].bitcast(F32)
+            for gp in range(2):
+                tb = transposes_into_bank(x32, 512 * gp, 256)
+                w0 = (4 * m + 2 * gp) * 256
+                drain_bank(gp == 0, xg32[:, w0:w0 + 512], tb)
+        nc.vector.quantize_mx(out=xc[:].bitcast(FP8X4), scales=xs[:], in_=xg[:])
+
+        banks = {}
+        grouped = {}
+        codes = {}
+        acc = {}
+        ytile = {}
+        stats = {}
+
+        def stage_t(k):
+            w32 = w_tiles[k][:].rearrange("p t k -> p (t k)").bitcast(F32)
+            for g in range(4):
+                banks[(k, g)] = transposes_into_bank(w32, 256 * g, 1024)
+            if k + W_AHEAD < NSLOT:
+                load_w(k + W_AHEAD)
+
+        def stage_d(k, g):
+            blk = k // 2
+            tt = k % 2
+            if tt == 0:
+                grouped[(blk, g)] = gpool.tile([P, 2048], BF16, name="grp", align_bytes=64)
+            g32 = grouped[(blk, g)][:].bitcast(F32)
+            drain_bank(g == 3, g32[:, 512 * tt:512 * (tt + 1)], banks[(k, g)])
+
+        def stage_q(blk, g):
+            cd = cpool.tile([P, 512], U32, name="cd", align_bytes=64)
+            sc = cpool.tile([P, 512], U8, name="sc", align_bytes=64)
+            nc.vector.quantize_mx(
+                out=cd[:].bitcast(FP8X4), scales=sc[:], in_=grouped[(blk, g)][:]
+            )
+            codes[(blk, g)] = (cd, sc)
+
+        def stage_m(blk, gp):
+            for m in range(2):
+                if gp == 0:
+                    acc[(blk, m)] = opsum.tile([P, 512], F32, name="acc")
+                for g in (2 * gp, 2 * gp + 1):
+                    cd, sc = codes[(blk, g)]
+                    xcol = (4 * m + g) * P
+                    nc.tensor.matmul_mx(
+                        out=acc[(blk, m)][:],
+                        lhsT=xc[:, xcol:xcol + P].bitcast(FP8X4),
+                        lhsT_scale=xs[:, xcol:xcol + P],
+                        rhs=cd[:].bitcast(FP8X4),
+                        rhs_scale=sc[:],
+                        start=(g == 0),
+                        stop=(g == 3),
+                    )
+
+        def qk_groups(i):
+            return [gq for gq in range(4) if (4 * i + gq) % 3 != 2]
+
+        def stage_a(i, m):
+            if i % 3 == 0:
+                ytile[(i // 3, m)] = ypool.tile([P, 1536], F32, name="y3")
+            off = 512 * (i % 3)
+            nc.vector.tensor_tensor(
+                out=ytile[(i // 3, m)][:, off:off + 512].rearrange("q (p t) -> q p t", t=4),
+                in0=acc[(i, m)][:].rearrange("q (t p) -> q p t", t=4),
+                in1=bias_bc[:, 512 * i:512 * (i + 1)].rearrange("q (p t) -> q p t", t=4),
+                op=ALU.add,
+            )
+
+        def group_ap(i, m, gq):
+            off = 512 * (i % 3) + P * gq
+            return ytile[(i // 3, m)][:, off:off + P]
+
+        def stage_sq(i, m, r):
+            groups = qk_groups(i)
+            n = len(groups)
+            if m == 0 and r == 0:
+                stats[(i, "ss")] = spool.tile([P, 2 * n], F32, name="ss")
+            sq = spool.tile([P, P], F32, name="sq")
+            col = m * n + r
+            nc.scalar.activation(
+                out=sq[:],
+                in_=group_ap(i, m, groups[r]),
+                func=ACT.Square,
+                accum_out=stats[(i, "ss")][:, col:col + 1],
+            )
+
+        def stage_max(i):
+            n = len(qk_groups(i))
+            stats[(i, "sc")] = spool.tile([P, 2 * n], F32, name="ssc")
+            nc.vector.tensor_scalar_max(
+                out=stats[(i, "sc")][:], in0=stats[(i, "ss")][:], scalar1=1e-24
+            )
+
+        def stage_sqrt(i):
+            n = len(qk_groups(i))
+            stats[(i, "nr")] = spool.tile([P, 2 * n], F32, name="nrm")
+            nc.scalar.sqrt(out=stats[(i, "nr")][:], in_=stats[(i, "sc")][:])
+
+        def stage_recip(i):
+            n = len(qk_groups(i))
+            stats[(i, "rn")] = spool.tile([P, 2 * n], F32, name="rn")
+            nc.vector.reciprocal(out=stats[(i, "rn")][:], in_=stats[(i, "nr")][:])
+
+        def stage_scale(i):
+            groups = qk_groups(i)
+            n = len(groups)
+            eng = nc.vector if i >= NBLK - 2 else nc.gpsimd
+            for m in range(2):
+                for r in range(n):
+                    ap = group_ap(i, m, groups[r])
+                    col = m * n + r
+                    eng.tensor_scalar(
+                        out=ap, in0=ap, scalar1=stats[(i, "rn")][:, col:col + 1],
+                        scalar2=0.0, op0=ALU.mult, op1=ALU.add,
+                    )
+
+        def flush(i, kinds):
+            if i % 3 != 2:
+                return
+            sb = i // 3
+            for s in kinds:
+                for m in range(2):
+                    for bl in range(2):
+                        view = ytile[(sb, m)][bl:P:2, :].rearrange(
+                            "q (h s c) -> q s h c", s=3, c=HD
+                        )
+                        nc.sync.dma_start(
+                            out=outs[s][2 * m + bl, 4 * sb:4 * sb + 4, :, :].rearrange(
+                                "h l c -> l h c"
+                            ),
+                            in_=view[:, s, :, :],
+                        )
+
+        def block_at(slot, lag):
+            v = slot - lag
+            if v >= 0 and v % 2 == 0 and v // 2 < NBLK:
+                return v // 2
+            return None
+
+        for k in range(NSLOT + 9):
+            i_rc = block_at(k, 8)
+            if i_rc is not None:
+                stage_recip(i_rc)
+                stage_scale(i_rc)
+                flush(i_rc, (0, 1))
+            i_mx = block_at(k, 7)
+            if i_mx is not None:
+                stage_max(i_mx)
+            i_a = block_at(k, 5)
+            if i_a is not None:
+                stage_a(i_a, 0)
+                stage_a(i_a, 1)
+                flush(i_a, (2,))
+            if k < NSLOT:
+                stage_t(k)
+            squares = []
+            if i_a is not None:
+                squares = [(i_a, 0, r) for r in range(len(qk_groups(i_a)))]
+            i_s1 = block_at(k, 6)
+            if i_s1 is not None:
+                squares = [(i_s1, 1, r) for r in range(len(qk_groups(i_s1)))]
+            if 0 <= k - 2 < NSLOT:
+                stage_q((k - 2) // 2, 2 * (k % 2))
+                stage_q((k - 2) // 2, 2 * (k % 2) + 1)
+            for j in range(4):
+                if k < NSLOT:
+                    stage_d(k, j)
+                if j < len(squares):
+                    stage_sq(*squares[j])
+            if i_mx is not None:
+                stage_sqrt(i_mx)
+            if 0 <= k - 3 < NSLOT:
+                stage_m((k - 3) // 2, (k - 3) % 2)

@@ -16,10 +16,24 @@ P = 128
 E = 2048
 NH = 16
 HD = 128
-NBLK = 12
-NSLOT = 2 * NBLK
+NSLOT = 24
 W_AHEAD = 12
 T_BANKS = 5
+N_SORTED = 3
+NV = 3
+HSB = 4
+BV = False
+LA = 4
+LSQ = 5
+LX = 6
+LC = 7
+RUN = 2
+VORD = "PRACXQ"
+SORD = "00r0101"
+FINE = 2
+FINEV = 2
+BIASDMA = 0
+GT = 0
 FLOPS = 2 * 256 * 2048 * 6144
 
 
@@ -29,9 +43,10 @@ def tile_selfattention_pa_kernel(tc, x, W, b, out_0, out_1, out_2):
     with ExitStack() as ctx:
         const = ctx.enter_context(tc.tile_pool(name="const", bufs=1))
         wpool = ctx.enter_context(tc.tile_pool(name="wpool", bufs=W_AHEAD))
-        gpool = ctx.enter_context(tc.tile_pool(name="gpool", bufs=8))
-        cpool = ctx.enter_context(tc.tile_pool(name="cpool", bufs=6))
-        ypool = ctx.enter_context(tc.tile_pool(name="ypool", bufs=6))
+        ppool = ctx.enter_context(tc.tile_pool(name="ppool", bufs=3))
+        gpool = ctx.enter_context(tc.tile_pool(name="gpool", bufs=12))
+        cpool = ctx.enter_context(tc.tile_pool(name="cpool", bufs=16))
+        ypool = ctx.enter_context(tc.tile_pool(name="ypool", bufs=3))
         spool = ctx.enter_context(tc.tile_pool(name="spool", bufs=4))
         tpsum = ctx.enter_context(tc.psum_pool(name="tpsum", bufs=T_BANKS))
         opsum = ctx.enter_context(tc.psum_pool(name="opsum", bufs=8 - T_BANKS))
@@ -48,24 +63,39 @@ def tile_selfattention_pa_kernel(tc, x, W, b, out_0, out_1, out_2):
         xc = const.tile([P, 1024], U32, name="xc", align_bytes=64)
         xs = const.tile([P, 1024], U8, name="xs", align_bytes=64)
 
+        def is_v(k):
+            return k % 6 >= HSB
+
+        def first_head(k):
+            return HSB * (k // 6) + (2 * (k % 6 - HSB) if is_v(k) else k % 6)
+
         w_tiles = {}
 
-        def load_w(k):
-            blk = k // 2
-            tt = k % 2
-            rows = W[512 * blk:512 * (blk + 1), :].rearrange("(p t) k -> p t k", t=4)
+        def w_rows(k):
+            r0 = 384 * first_head(k)
+            if is_v(k):
+                return W[r0:r0 + 768, :].rearrange("(t r p) k -> r p t k", t=2, r=3)[2]
+            return W[r0:r0 + 256, :].rearrange("(p t) k -> p t k", t=2)
+
+        def load_w(k, pieces):
             w_sb = wpool.tile([P, 2, E], BF16, name="w_sb")
-            nc.sync.dma_start(out=w_sb[:], in_=rows[:, 2 * tt:2 * tt + 2, :])
+            rows = w_rows(k)
+            n = E // pieces
+            for j in range(pieces):
+                nc.sync.dma_start(
+                    out=w_sb[:, :, n * j:n * (j + 1)], in_=rows[:, :, n * j:n * (j + 1)]
+                )
             w_tiles[k] = w_sb
 
         nc.vector.memset(b_sb[:].bitcast(I32), 0)
         nc.vector.memset(warm[:], 1.0)
         nc.sync.dma_start(out=b_sb[0:16, :], in_=b.rearrange("(h n) -> h n", h=16))
+        load_w(0, 2)
         for m in range(2):
             for bl in range(2):
                 nc.sync.dma_start(out=x_sb[m][bl:P:2, :], in_=x[2 * m + bl, :, :])
-        for k in range(W_AHEAD):
-            load_w(k)
+        for k in range(1, W_AHEAD):
+            load_w(k, 1)
         make_identity(nc, ident_b[:])
         make_identity(nc, ident_f[:])
         nc.scalar.sqrt(out=warm2[:], in_=warm[:])
@@ -76,44 +106,51 @@ def tile_selfattention_pa_kernel(tc, x, W, b, out_0, out_1, out_2):
             else:
                 nc.scalar.copy(out=dst, in_=src)
 
-        for h in range(NH):
-            tb = tpsum.tile([P, 512], F32, name="tb")
-            nc.tensor.matmul(
-                out=tb[:, 0:384],
-                lhsT=ident_b[:, h:h + 1].to_broadcast([P, P]),
-                rhs=b_sb[:],
-                start=True,
-                stop=True,
-            )
-            drain(h % 2 == 0, bias_bc[:, 384 * h:384 * (h + 1)], tb[:, 0:384])
+        def bias_pair(j, on_vector):
+            tb = tpsum.tile([P, 1024], BF16, name="tb")
+            for h in (2 * j, 2 * j + 1):
+                c0 = 384 * (h - 2 * j)
+                nc.tensor.matmul(
+                    out=tb[:, c0:c0 + 384],
+                    lhsT=ident_b[:, h:h + 1].to_broadcast([P, P]),
+                    rhs=b_sb[:],
+                    start=True,
+                    stop=True,
+                )
+            drain(on_vector, bias_bc[:, 768 * j:768 * (j + 1)], tb[:, 0:768])
 
-        def transposes_into_bank(src32, col0, step_a):
+        def stepped_words(src32, c0):
+            return [src32[:, c0 + u:c0 + u + 2 * P - 1:2] for u in range(2)]
+
+        def transposes_into_bank(operands):
             tb = tpsum.tile([P, 512], F32, name="tb")
-            for a in range(2):
-                for u in range(2):
-                    c0 = col0 + a * step_a + u
-                    nc.tensor.transpose(
-                        out=tb[:, (2 * a + u) * P:(2 * a + u + 1) * P],
-                        in_=src32[:, c0:c0 + 2 * P - 1:2],
-                        identity=ident_f[:],
-                    )
+            for j, op in enumerate(operands):
+                nc.tensor.transpose(
+                    out=tb[:, j * P:(j + 1) * P], in_=op, identity=ident_f[:]
+                )
             return tb
 
-        def drain_bank(on_vector, dst32, tb):
-            drain(
-                on_vector,
-                dst32.rearrange("q (a c u) -> q a c u", a=2, u=2),
-                tb[:].rearrange("q (a u c) -> q a c u", a=2, u=2),
-            )
-
         xg32 = xg[:].bitcast(F32)
-        for m in range(2):
+
+        def stage_x(m, on_vector):
             x32 = x_sb[m][:].bitcast(F32)
             for gp in range(2):
-                tb = transposes_into_bank(x32, 512 * gp, 256)
+                tb = transposes_into_bank(
+                    stepped_words(x32, 512 * gp) + stepped_words(x32, 512 * gp + 256)
+                )
                 w0 = (4 * m + 2 * gp) * 256
-                drain_bank(gp == 0, xg32[:, w0:w0 + 512], tb)
-        nc.vector.quantize_mx(out=xc[:].bitcast(FP8X4), scales=xs[:], in_=xg[:])
+                drain(
+                    on_vector,
+                    xg32[:, w0:w0 + 512].rearrange("q (a c u) -> q a c u", a=2, u=2),
+                    tb[:].rearrange("q (a u c) -> q a c u", a=2, u=2),
+                )
+
+        def stage_xq(m):
+            nc.vector.quantize_mx(
+                out=xc[:, 512 * m:512 * (m + 1)].bitcast(FP8X4),
+                scales=xs[:, 512 * m:512 * (m + 1)],
+                in_=xg[:, 2048 * m:2048 * (m + 1)],
+            )
 
         banks = {}
         grouped = {}
@@ -121,39 +158,68 @@ def tile_selfattention_pa_kernel(tc, x, W, b, out_0, out_1, out_2):
         acc = {}
         ytile = {}
         stats = {}
+        sorted_words = {}
+
+        def n_sorted(k):
+            return 0 if k == 0 else (NV if is_v(k) else N_SORTED)
+
+        def stage_p(k):
+            n = n_sorted(k)
+            if n == 0:
+                return
+            srt = ppool.tile([P, 2, 2, n * P], F32, name="srt")
+            w32 = w_tiles[k][:].rearrange("p t k -> p (t k)").bitcast(F32)
+            nc.vector.tensor_copy(
+                out=srt[:],
+                in_=w32.rearrange("p (a w) -> p a w", a=2)[:, :, 0:256 * n].rearrange(
+                    "p a (w u) -> p a u w", u=2
+                ),
+            )
+            sorted_words[k] = srt
 
         def stage_t(k):
             w32 = w_tiles[k][:].rearrange("p t k -> p (t k)").bitcast(F32)
             for g in range(4):
-                banks[(k, g)] = transposes_into_bank(w32, 256 * g, 1024)
+                if g < n_sorted(k):
+                    ops = [
+                        sorted_words[k][:, a, u, g * P:(g + 1) * P]
+                        for a in range(2) for u in range(2)
+                    ]
+                else:
+                    ops = stepped_words(w32, 256 * g) + stepped_words(w32, 1024 + 256 * g)
+                banks[(k, g)] = transposes_into_bank(ops)
             if k + W_AHEAD < NSLOT:
-                load_w(k + W_AHEAD)
+                load_w(k + W_AHEAD, 1)
 
-        def stage_d(k, g):
-            blk = k // 2
-            tt = k % 2
-            if tt == 0:
-                grouped[(blk, g)] = gpool.tile([P, 2048], BF16, name="grp", align_bytes=64)
-            g32 = grouped[(blk, g)][:].bitcast(F32)
-            drain_bank(g == 3, g32[:, 512 * tt:512 * (tt + 1)], banks[(k, g)])
+        def stage_d(k, g, on_vector):
+            grp = gpool.tile([P, 1024], BF16, name="grp", align_bytes=64)
+            grouped[(k, g)] = grp
+            src = banks[(k, g)][:]
+            dst = grp[:].bitcast(F32)
+            if is_v(k):
+                dst = dst.rearrange("q (a c u) -> q a c u", a=2, u=2)
+                src = src.rearrange("q (a u c) -> q a c u", a=2, u=2)
+            else:
+                dst = dst.rearrange("q (c a u) -> q c a u", a=2, u=2)
+                src = src.rearrange("q (a u c) -> q c a u", a=2, u=2)
+            drain(on_vector, dst, src)
 
-        def stage_q(blk, g):
-            cd = cpool.tile([P, 512], U32, name="cd", align_bytes=64)
-            sc = cpool.tile([P, 512], U8, name="sc", align_bytes=64)
+        def stage_q(k, g):
+            cd = cpool.tile([P, 256], U32, name="cd", align_bytes=64)
+            sc = cpool.tile([P, 256], U8, name="sc", align_bytes=64)
             nc.vector.quantize_mx(
-                out=cd[:].bitcast(FP8X4), scales=sc[:], in_=grouped[(blk, g)][:]
+                out=cd[:].bitcast(FP8X4), scales=sc[:], in_=grouped[(k, g)][:]
             )
-            codes[(blk, g)] = (cd, sc)
+            codes[(k, g)] = (cd, sc)
 
-        def stage_m(blk, gp):
+        def stage_m(k):
+            acc[k] = opsum.tile([P, 512], F32, name="acc")
             for m in range(2):
-                if gp == 0:
-                    acc[(blk, m)] = opsum.tile([P, 512], F32, name="acc")
-                for g in (2 * gp, 2 * gp + 1):
-                    cd, sc = codes[(blk, g)]
+                for g in range(4):
+                    cd, sc = codes[(k, g)]
                     xcol = (4 * m + g) * P
                     nc.tensor.matmul_mx(
-                        out=acc[(blk, m)][:],
+                        out=acc[k][:, 256 * m:256 * (m + 1)],
                         lhsT=xc[:, xcol:xcol + P].bitcast(FP8X4),
                         lhsT_scale=xs[:, xcol:xcol + P],
                         rhs=cd[:].bitcast(FP8X4),
@@ -162,122 +228,176 @@ def tile_selfattention_pa_kernel(tc, x, W, b, out_0, out_1, out_2):
                         stop=(g == 3),
                     )
 
-        def qk_groups(i):
-            return [gq for gq in range(4) if (4 * i + gq) % 3 != 2]
+        def y_part(k):
+            h = first_head(k)
+            y = ytile[h // HSB]
+            hl = h % HSB
+            if is_v(k):
+                return y[:, :, 2, hl:hl + 2, :]
+            return y[:, :, 0:2, hl, :]
 
-        def stage_a(i, m):
-            if i % 3 == 0:
-                ytile[(i // 3, m)] = ypool.tile([P, 1536], F32, name="y3")
-            off = 512 * (i % 3)
+        def stage_a(k):
+            h = first_head(k)
+            if h % HSB == 0 and not is_v(k):
+                ytile[h // HSB] = ypool.tile([P, 2, 3, HSB, HD], F32, name="y")
+            if is_v(k):
+                bias = bias_bc[:, 384 * h:384 * h + 768].rearrange(
+                    "q (g s c) -> q s g c", g=2, s=3
+                )[:, 2]
+            else:
+                bias = bias_bc[:, 384 * h:384 * h + 256].rearrange("q (g c) -> q g c", g=2)
             nc.vector.tensor_tensor(
-                out=ytile[(i // 3, m)][:, off:off + 512].rearrange("q (p t) -> q p t", t=4),
-                in0=acc[(i, m)][:].rearrange("q (t p) -> q p t", t=4),
-                in1=bias_bc[:, 512 * i:512 * (i + 1)].rearrange("q (p t) -> q p t", t=4),
+                out=y_part(k),
+                in0=acc[k][:].rearrange("q (m g c) -> q m g c", m=2, g=2),
+                in1=bias.unsqueeze(1).to_broadcast([P, 2, 2, HD]),
                 op=ALU.add,
             )
 
-        def group_ap(i, m, gq):
-            off = 512 * (i % 3) + P * gq
-            return ytile[(i // 3, m)][:, off:off + P]
+        def norm_ap(k, j):
+            h = first_head(k)
+            return ytile[h // HSB][:, j // 2, j % 2, h % HSB, :]
 
-        def stage_sq(i, m, r):
-            groups = qk_groups(i)
-            n = len(groups)
-            if m == 0 and r == 0:
-                stats[(i, "ss")] = spool.tile([P, 2 * n], F32, name="ss")
+        def stage_sq(k, j):
+            if j == 0:
+                stats[(k, "ss")] = spool.tile([P, 4], F32, name="ss")
             sq = spool.tile([P, P], F32, name="sq")
-            col = m * n + r
             nc.scalar.activation(
-                out=sq[:],
-                in_=group_ap(i, m, groups[r]),
-                func=ACT.Square,
-                accum_out=stats[(i, "ss")][:, col:col + 1],
+                out=sq[:], in_=norm_ap(k, j), func=ACT.Square,
+                accum_out=stats[(k, "ss")][:, j:j + 1],
             )
 
-        def stage_max(i):
-            n = len(qk_groups(i))
-            stats[(i, "sc")] = spool.tile([P, 2 * n], F32, name="ssc")
+        def stage_max(k):
+            stats[(k, "sc")] = spool.tile([P, 4], F32, name="ssc")
             nc.vector.tensor_scalar_max(
-                out=stats[(i, "sc")][:], in0=stats[(i, "ss")][:], scalar1=1e-24
+                out=stats[(k, "sc")][:], in0=stats[(k, "ss")][:], scalar1=1e-24
             )
 
-        def stage_sqrt(i):
-            n = len(qk_groups(i))
-            stats[(i, "nr")] = spool.tile([P, 2 * n], F32, name="nrm")
-            nc.scalar.sqrt(out=stats[(i, "nr")][:], in_=stats[(i, "sc")][:])
+        def stage_sqrt(k):
+            stats[(k, "nr")] = spool.tile([P, 4], F32, name="nrm")
+            nc.scalar.sqrt(out=stats[(k, "nr")][:], in_=stats[(k, "sc")][:])
 
-        def stage_recip(i):
-            n = len(qk_groups(i))
-            stats[(i, "rn")] = spool.tile([P, 2 * n], F32, name="rn")
-            nc.vector.reciprocal(out=stats[(i, "rn")][:], in_=stats[(i, "nr")][:])
+        def stage_recip(k):
+            rn = spool.tile([P, 4], F32, name="rn")
+            nc.vector.reciprocal(out=rn[:], in_=stats[(k, "nr")][:])
+            stats[(k, "rn")] = rn
 
-        def stage_scale(i):
-            groups = qk_groups(i)
-            n = len(groups)
-            eng = nc.vector if i >= NBLK - 2 else nc.gpsimd
+        def stage_scale(k):
+            rn = stats[(k, "rn")]
+            for j in range(4):
+                nc.vector.tensor_scalar(
+                    out=norm_ap(k, j), in0=norm_ap(k, j), scalar1=rn[:, j:j + 1],
+                    scalar2=None, op0=ALU.mult,
+                )
+
+        def store(s, h0, n):
+            y = ytile[h0 // HSB]
+            hl = h0 % HSB
             for m in range(2):
-                for r in range(n):
-                    ap = group_ap(i, m, groups[r])
-                    col = m * n + r
-                    eng.tensor_scalar(
-                        out=ap, in0=ap, scalar1=stats[(i, "rn")][:, col:col + 1],
-                        scalar2=0.0, op0=ALU.mult, op1=ALU.add,
+                for bl in range(2):
+                    nc.sync.dma_start(
+                        out=outs[s][2 * m + bl, h0:h0 + n, :, :].rearrange("h l c -> l h c"),
+                        in_=y[bl:P:2, m, s, hl:hl + n, :],
                     )
 
-        def flush(i, kinds):
-            if i % 3 != 2:
-                return
-            sb = i // 3
-            for s in kinds:
-                for m in range(2):
-                    for bl in range(2):
-                        view = ytile[(sb, m)][bl:P:2, :].rearrange(
-                            "q (h s c) -> q s h c", s=3, c=HD
-                        )
-                        nc.sync.dma_start(
-                            out=outs[s][2 * m + bl, 4 * sb:4 * sb + 4, :, :].rearrange(
-                                "h l c -> l h c"
-                            ),
-                            in_=view[:, s, :, :],
-                        )
+        def active(k):
+            return 0 <= k < NSLOT
 
-        def block_at(slot, lag):
-            v = slot - lag
-            if v >= 0 and v % 2 == 0 and v // 2 < NBLK:
-                return v // 2
-            return None
+        def active_qk(k):
+            return active(k) and not is_v(k)
 
-        for k in range(NSLOT + 9):
-            i_rc = block_at(k, 8)
-            if i_rc is not None:
-                stage_recip(i_rc)
-                stage_scale(i_rc)
-                flush(i_rc, (0, 1))
-            i_mx = block_at(k, 7)
-            if i_mx is not None:
-                stage_max(i_mx)
-            i_a = block_at(k, 5)
-            if i_a is not None:
-                stage_a(i_a, 0)
-                stage_a(i_a, 1)
-                flush(i_a, (2,))
-            if k < NSLOT:
-                stage_t(k)
-            squares = []
-            if i_a is not None:
-                squares = [(i_a, 0, r) for r in range(len(qk_groups(i_a)))]
-            i_s1 = block_at(k, 6)
-            if i_s1 is not None:
-                squares = [(i_s1, 1, r) for r in range(len(qk_groups(i_s1)))]
-            if 0 <= k - 2 < NSLOT:
-                stage_q((k - 2) // 2, 2 * (k % 2))
-                stage_q((k - 2) // 2, 2 * (k % 2) + 1)
-            for j in range(4):
-                if k < NSLOT:
-                    stage_d(k, j)
-                if j < len(squares):
-                    stage_sq(*squares[j])
-            if i_mx is not None:
-                stage_sqrt(i_mx)
-            if 0 <= k - 3 < NSLOT:
-                stage_m((k - 3) // 2, (k - 3) % 2)
+        if not BIASDMA:
+            bias_pair(0, True)
+            bias_pair(1, False)
+        nxt = {"A": 0, "S": 0, "X": 0, "r": 0, "R": 0, "C": 0, "M": 0}
+
+        def run(stage, last, fn):
+            while nxt[stage] <= min(last, NSLOT - 1):
+                j = nxt[stage]
+                nxt[stage] = j + 1
+                if stage in ("A", "M") or not is_v(j):
+                    fn(j)
+
+        def do_a(j):
+            stage_a(j)
+            h = first_head(j)
+            n = HSB if h < NH - HSB else FINEV
+            if is_v(j) and (h + 2) % n == 0:
+                store(2, h + 2 - n, n)
+
+        def do_c(j):
+            stage_scale(j)
+            h = first_head(j)
+            n = HSB if h < NH - HSB else FINE
+            if (h + 1) % n == 0:
+                store(0, h + 1 - n, n)
+                store(1, h + 1 - n, n)
+
+        for k in range(NSLOT):
+            stage_t(k)
+            if k == 0:
+                stage_d(k, 0, False)
+                stage_d(k, 1, True)
+                stage_d(k, 2, False)
+                stage_d(k, 3, True)
+                if not BIASDMA:
+                    bias_pair(2, True)
+                    bias_pair(3, True)
+                stage_x(0, False)
+                stage_x(1, True)
+            for c in VORD:
+                if c == "A":
+                    run("A", k - LA, do_a)
+                if c == "R":
+                    run("R", k - LC, stage_recip)
+                if c == "C":
+                    run("C", k - LC, do_c)
+                if c == "X":
+                    run("X", k - LX, stage_max)
+                if c == "P":
+                    if k + 1 < NSLOT:
+                        stage_p(k + 1)
+                    if k == 1:
+                        stage_xq(0)
+                        stage_xq(1)
+                if c == "Q" and k > 0:
+                    for g in range(4):
+                        stage_q(k - 1, g)
+            nd = 0
+            sqs = []
+            run("S", k - LSQ, sqs.append)
+            pieces = [(j, i) for j in sqs for i in range(4)]
+            for c in SORD:
+                if c == "0":
+                    if k > 0:
+                        stage_d(k, nd, False)
+                    nd += 1
+                if c == "1":
+                    for j, i in pieces[0:2]:
+                        stage_sq(j, i)
+                    pieces = pieces[2:]
+                if c == "r":
+                    run("r", k - LX, stage_sqrt)
+            for j, i in pieces:
+                stage_sq(j, i)
+            if k in (1, 2) and not BIASDMA:
+                bias_pair(2 * k + 2, BV)
+                bias_pair(2 * k + 3, BV)
+            if k % RUN == RUN - 1:
+                run("M", k - 2, stage_m)
+
+        last = NSLOT - 1
+        for g in range(4):
+            stage_q(last, g)
+        run("M", last, stage_m)
+
+        def square_all(j):
+            for i in range(4):
+                stage_sq(j, i)
+
+        for j in range(nxt["A"], NSLOT):
+            run("A", j, do_a)
+            run("S", j, square_all)
+            run("X", j - GT, stage_max)
+            run("r", j - GT, stage_sqrt)
+            run("R", j - GT, stage_recip)
+            run("C", j - GT, do_c)

@@ -23,11 +23,11 @@ N_SORTED = 3
 NV = 3
 HSB = 4
 BV = False
-LA = 4
-LSQ = 5
-LX = 6
-LC = 7
-RUN = 2
+LA = 3
+LSQ = 4
+LX = 5
+LC = 6
+RUN = 1
 VORD = "PRACXQ"
 SORD = "00r0101"
 FINE = 2
@@ -45,7 +45,7 @@ def tile_selfattention_pa_kernel(tc, x, W, b, out_0, out_1, out_2):
         wpool = ctx.enter_context(tc.tile_pool(name="wpool", bufs=W_AHEAD))
         ppool = ctx.enter_context(tc.tile_pool(name="ppool", bufs=3))
         gpool = ctx.enter_context(tc.tile_pool(name="gpool", bufs=12))
-        cpool = ctx.enter_context(tc.tile_pool(name="cpool", bufs=16))
+        cpool = ctx.enter_context(tc.tile_pool(name="cpool", bufs=12))
         ypool = ctx.enter_context(tc.tile_pool(name="ypool", bufs=3))
         spool = ctx.enter_context(tc.tile_pool(name="spool", bufs=4))
         tpsum = ctx.enter_context(tc.psum_pool(name="tpsum", bufs=T_BANKS))
@@ -75,7 +75,7 @@ def tile_selfattention_pa_kernel(tc, x, W, b, out_0, out_1, out_2):
             r0 = 384 * first_head(k)
             if is_v(k):
                 return W[r0:r0 + 768, :].rearrange("(t r p) k -> r p t k", t=2, r=3)[2]
-            return W[r0:r0 + 256, :].rearrange("(p t) k -> p t k", t=2)
+            return W[r0:r0 + 256, :].rearrange("(t p) k -> p t k", t=2)
 
         def load_w(k, pieces):
             w_sb = wpool.tile([P, 2, E], BF16, name="w_sb")
@@ -196,13 +196,11 @@ def tile_selfattention_pa_kernel(tc, x, W, b, out_0, out_1, out_2):
             grouped[(k, g)] = grp
             src = banks[(k, g)][:]
             dst = grp[:].bitcast(F32)
-            if is_v(k):
-                dst = dst.rearrange("q (a c u) -> q a c u", a=2, u=2)
-                src = src.rearrange("q (a u c) -> q a c u", a=2, u=2)
-            else:
-                dst = dst.rearrange("q (c a u) -> q c a u", a=2, u=2)
-                src = src.rearrange("q (a u c) -> q c a u", a=2, u=2)
-            drain(on_vector, dst, src)
+            drain(
+                on_vector,
+                dst.rearrange("q (a c u) -> q a c u", a=2, u=2),
+                src.rearrange("q (a u c) -> q a c u", a=2, u=2),
+            )
 
         def stage_q(k, g):
             cd = cpool.tile([P, 256], U32, name="cd", align_bytes=64)

@@ -17,10 +17,8 @@ E = 2048
 NH = 16
 HD = 128
 NSLOT = 24
-W_AHEAD = 12
+W_AHEAD = 11
 T_BANKS = 5
-N_SORTED = 3
-NV = 3
 HSB = 4
 BV = False
 LA = 3
@@ -28,7 +26,7 @@ LSQ = 4
 LX = 5
 LC = 6
 RUN = 1
-VORD = "PRACXQ"
+VORD = "PACQ"
 SORD = "00r0101"
 FINE = 2
 FINEV = 2
@@ -59,6 +57,7 @@ def tile_selfattention_pa_kernel(tc, x, W, b, out_0, out_1, out_2):
         warm = const.tile([P, 1], F32, name="warm")
         warm2 = const.tile([P, 1], F32, name="warm2")
         x_sb = [const.tile([P, E], BF16, name="x_sb%d" % m) for m in range(2)]
+        xsort = [const.tile([P, 2, 512], F32, name="xsort%d" % m) for m in range(2)]
         xg = const.tile([P, 4096], BF16, name="xg", align_bytes=64)
         xc = const.tile([P, 1024], U32, name="xc", align_bytes=64)
         xs = const.tile([P, 1024], U8, name="xs", align_bytes=64)
@@ -98,7 +97,7 @@ def tile_selfattention_pa_kernel(tc, x, W, b, out_0, out_1, out_2):
             load_w(k, 1)
         make_identity(nc, ident_b[:])
         make_identity(nc, ident_f[:])
-        nc.scalar.sqrt(out=warm2[:], in_=warm[:])
+        nc.scalar.activation(out=warm2[:], in_=warm[:], func=ACT.Abs_reciprocal_sqrt)
 
         def drain(on_vector, dst, src):
             if on_vector:
@@ -119,9 +118,6 @@ def tile_selfattention_pa_kernel(tc, x, W, b, out_0, out_1, out_2):
                 )
             drain(on_vector, bias_bc[:, 768 * j:768 * (j + 1)], tb[:, 0:768])
 
-        def stepped_words(src32, c0):
-            return [src32[:, c0 + u:c0 + u + 2 * P - 1:2] for u in range(2)]
-
         def transposes_into_bank(operands):
             tb = tpsum.tile([P, 512], F32, name="tb")
             for j, op in enumerate(operands):
@@ -133,10 +129,13 @@ def tile_selfattention_pa_kernel(tc, x, W, b, out_0, out_1, out_2):
         xg32 = xg[:].bitcast(F32)
 
         def stage_x(m, on_vector):
-            x32 = x_sb[m][:].bitcast(F32)
+            srt = xsort[m]
             for gp in range(2):
                 tb = transposes_into_bank(
-                    stepped_words(x32, 512 * gp) + stepped_words(x32, 512 * gp + 256)
+                    [
+                        srt[:, u, P * g:P * (g + 1)]
+                        for g in (2 * gp, 2 * gp + 1) for u in range(2)
+                    ]
                 )
                 w0 = (4 * m + 2 * gp) * 256
                 drain(
@@ -160,34 +159,34 @@ def tile_selfattention_pa_kernel(tc, x, W, b, out_0, out_1, out_2):
         stats = {}
         sorted_words = {}
 
-        def n_sorted(k):
-            return 0 if k == 0 else (NV if is_v(k) else N_SORTED)
+        def sort_words(eng_v, dst, src):
+            d = dst.rearrange("p u (j i) -> p u j i", i=8)
+            s = src.rearrange("p (j u i) -> p u j i", u=2, i=8)
+            drain(eng_v, d, s)
 
         def stage_p(k):
-            n = n_sorted(k)
-            if n == 0:
-                return
-            srt = ppool.tile([P, 2, 2, n * P], F32, name="srt")
+            srt = ppool.tile([P, 2, 1024], F32, name="srt")
             w32 = w_tiles[k][:].rearrange("p t k -> p (t k)").bitcast(F32)
-            nc.vector.tensor_copy(
-                out=srt[:],
-                in_=w32.rearrange("p (a w) -> p a w", a=2)[:, :, 0:256 * n].rearrange(
-                    "p a (w u) -> p a u w", u=2
-                ),
-            )
+            if k == 0:
+                for a in range(2):
+                    for h in range(2):
+                        w0 = 1024 * a + 512 * h
+                        sort_words(
+                            a == 0, srt[:, :, w0 // 2:w0 // 2 + 256], w32[:, w0:w0 + 512]
+                        )
+            else:
+                sort_words(True, srt[:], w32)
             sorted_words[k] = srt
 
         def stage_t(k):
-            w32 = w_tiles[k][:].rearrange("p t k -> p (t k)").bitcast(F32)
+            srt = sorted_words[k]
             for g in range(4):
-                if g < n_sorted(k):
-                    ops = [
-                        sorted_words[k][:, a, u, g * P:(g + 1) * P]
+                banks[(k, g)] = transposes_into_bank(
+                    [
+                        srt[:, u, 512 * a + P * g:512 * a + P * (g + 1)]
                         for a in range(2) for u in range(2)
                     ]
-                else:
-                    ops = stepped_words(w32, 256 * g) + stepped_words(w32, 1024 + 256 * g)
-                banks[(k, g)] = transposes_into_bank(ops)
+                )
             if k + W_AHEAD < NSLOT:
                 load_w(k + W_AHEAD, 1)
 
@@ -266,18 +265,16 @@ def tile_selfattention_pa_kernel(tc, x, W, b, out_0, out_1, out_2):
 
         def stage_max(k):
             stats[(k, "sc")] = spool.tile([P, 4], F32, name="ssc")
-            nc.vector.tensor_scalar_max(
+            nc.gpsimd.tensor_scalar_max(
                 out=stats[(k, "sc")][:], in0=stats[(k, "ss")][:], scalar1=1e-24
             )
 
-        def stage_sqrt(k):
-            stats[(k, "nr")] = spool.tile([P, 4], F32, name="nrm")
-            nc.scalar.sqrt(out=stats[(k, "nr")][:], in_=stats[(k, "sc")][:])
-
-        def stage_recip(k):
-            rn = spool.tile([P, 4], F32, name="rn")
-            nc.vector.reciprocal(out=rn[:], in_=stats[(k, "nr")][:])
-            stats[(k, "rn")] = rn
+        def stage_rsqrt(k):
+            stats[(k, "rn")] = spool.tile([P, 4], F32, name="rn")
+            nc.scalar.activation(
+                out=stats[(k, "rn")][:], in_=stats[(k, "sc")][:],
+                func=ACT.Abs_reciprocal_sqrt,
+            )
 
         def stage_scale(k):
             rn = stats[(k, "rn")]
@@ -330,8 +327,12 @@ def tile_selfattention_pa_kernel(tc, x, W, b, out_0, out_1, out_2):
                 store(0, h + 1 - n, n)
                 store(1, h + 1 - n, n)
 
+        stage_p(0)
         for k in range(NSLOT):
             stage_t(k)
+            if k == 0:
+                for m in range(2):
+                    sort_words(m == 1, xsort[m][:], x_sb[m][:].bitcast(F32))
             if k == 0:
                 stage_d(k, 0, False)
                 stage_d(k, 1, True)
@@ -345,12 +346,8 @@ def tile_selfattention_pa_kernel(tc, x, W, b, out_0, out_1, out_2):
             for c in VORD:
                 if c == "A":
                     run("A", k - LA, do_a)
-                if c == "R":
-                    run("R", k - LC, stage_recip)
                 if c == "C":
                     run("C", k - LC, do_c)
-                if c == "X":
-                    run("X", k - LX, stage_max)
                 if c == "P":
                     if k + 1 < NSLOT:
                         stage_p(k + 1)
@@ -374,7 +371,8 @@ def tile_selfattention_pa_kernel(tc, x, W, b, out_0, out_1, out_2):
                         stage_sq(j, i)
                     pieces = pieces[2:]
                 if c == "r":
-                    run("r", k - LX, stage_sqrt)
+                    run("X", k - LX, stage_max)
+                    run("r", k - LX, stage_rsqrt)
             for j, i in pieces:
                 stage_sq(j, i)
             if k in (1, 2) and not BIASDMA:
@@ -396,6 +394,5 @@ def tile_selfattention_pa_kernel(tc, x, W, b, out_0, out_1, out_2):
             run("A", j, do_a)
             run("S", j, square_all)
             run("X", j - GT, stage_max)
-            run("r", j - GT, stage_sqrt)
-            run("R", j - GT, stage_recip)
+            run("r", j - GT, stage_rsqrt)
             run("C", j - GT, do_c)

@@ -17,19 +17,28 @@ E = 2048
 NH = 16
 HD = 128
 NSLOT = 24
-W_AHEAD = 11
+W_AHEAD = 12
 T_BANKS = 5
 HSB = 4
+QKG = (16,)
 BV = False
 LA = 3
-LSQ = 4
-LX = 5
-LC = 6
+LSQ = 3
+LX = 4
+LC = 5
 RUN = 1
+XQ1 = False
+YB = 4
+SV = 0
+SQK = 0
+SPLIT = True
+CS = 1
+DV = True
+XV = True
 VORD = "PACQ"
-SORD = "00r0101"
+SORD = "000r101"
 FINE = 2
-FINEV = 2
+FINEV = 4
 BIASDMA = 0
 GT = 0
 FLOPS = 2 * 256 * 2048 * 6144
@@ -44,7 +53,7 @@ def tile_selfattention_pa_kernel(tc, x, W, b, out_0, out_1, out_2):
         ppool = ctx.enter_context(tc.tile_pool(name="ppool", bufs=3))
         gpool = ctx.enter_context(tc.tile_pool(name="gpool", bufs=12))
         cpool = ctx.enter_context(tc.tile_pool(name="cpool", bufs=12))
-        ypool = ctx.enter_context(tc.tile_pool(name="ypool", bufs=3))
+        ypool = ctx.enter_context(tc.tile_pool(name="ypool", bufs=YB))
         spool = ctx.enter_context(tc.tile_pool(name="spool", bufs=4))
         tpsum = ctx.enter_context(tc.psum_pool(name="tpsum", bufs=T_BANKS))
         opsum = ctx.enter_context(tc.psum_pool(name="opsum", bufs=8 - T_BANKS))
@@ -56,17 +65,21 @@ def tile_selfattention_pa_kernel(tc, x, W, b, out_0, out_1, out_2):
         bias_bc = const.tile([P, 6144], BF16, name="bias_bc")
         warm = const.tile([P, 1], F32, name="warm")
         warm2 = const.tile([P, 1], F32, name="warm2")
-        x_sb = [const.tile([P, E], BF16, name="x_sb%d" % m) for m in range(2)]
-        xsort = [const.tile([P, 2, 512], F32, name="xsort%d" % m) for m in range(2)]
-        xg = const.tile([P, 4096], BF16, name="xg", align_bytes=64)
         xc = const.tile([P, 1024], U32, name="xc", align_bytes=64)
         xs = const.tile([P, 1024], U8, name="xs", align_bytes=64)
 
+        slots = []
+        h0 = 0
+        for n in QKG:
+            slots += [(h, False) for h in range(h0, h0 + n)]
+            slots += [(h, True) for h in range(h0, h0 + n, 2)]
+            h0 += n
+
         def is_v(k):
-            return k % 6 >= HSB
+            return slots[k][1]
 
         def first_head(k):
-            return HSB * (k // 6) + (2 * (k % 6 - HSB) if is_v(k) else k % 6)
+            return slots[k][0]
 
         w_tiles = {}
 
@@ -90,10 +103,11 @@ def tile_selfattention_pa_kernel(tc, x, W, b, out_0, out_1, out_2):
         nc.vector.memset(warm[:], 1.0)
         nc.sync.dma_start(out=b_sb[0:16, :], in_=b.rearrange("(h n) -> h n", h=16))
         load_w(0, 2)
+        x_sb = wpool.tile([P, 2, E], BF16, name="w_sb")
         for m in range(2):
             for bl in range(2):
-                nc.sync.dma_start(out=x_sb[m][bl:P:2, :], in_=x[2 * m + bl, :, :])
-        for k in range(1, W_AHEAD):
+                nc.sync.dma_start(out=x_sb[bl:P:2, m, :], in_=x[2 * m + bl, :, :])
+        for k in range(1, W_AHEAD - 1):
             load_w(k, 1)
         make_identity(nc, ident_b[:])
         make_identity(nc, ident_f[:])
@@ -126,30 +140,32 @@ def tile_selfattention_pa_kernel(tc, x, W, b, out_0, out_1, out_2):
                 )
             return tb
 
-        xg32 = xg[:].bitcast(F32)
+        xgrp = {}
 
         def stage_x(m, on_vector):
-            srt = xsort[m]
             for gp in range(2):
                 tb = transposes_into_bank(
                     [
-                        srt[:, u, P * g:P * (g + 1)]
+                        xsort[:, u, 512 * m + P * g:512 * m + P * (g + 1)]
                         for g in (2 * gp, 2 * gp + 1) for u in range(2)
                     ]
                 )
-                w0 = (4 * m + 2 * gp) * 256
+                grp = gpool.tile([P, 1024], BF16, name="grp", align_bytes=64)
+                xgrp[(m, gp)] = grp
                 drain(
                     on_vector,
-                    xg32[:, w0:w0 + 512].rearrange("q (a c u) -> q a c u", a=2, u=2),
+                    grp[:].bitcast(F32).rearrange("q (a c u) -> q a c u", a=2, u=2),
                     tb[:].rearrange("q (a u c) -> q a c u", a=2, u=2),
                 )
 
         def stage_xq(m):
-            nc.vector.quantize_mx(
-                out=xc[:, 512 * m:512 * (m + 1)].bitcast(FP8X4),
-                scales=xs[:, 512 * m:512 * (m + 1)],
-                in_=xg[:, 2048 * m:2048 * (m + 1)],
-            )
+            for gp in range(2):
+                c0 = 512 * m + 256 * gp
+                nc.vector.quantize_mx(
+                    out=xc[:, c0:c0 + 256].bitcast(FP8X4),
+                    scales=xs[:, c0:c0 + 256],
+                    in_=xgrp[(m, gp)][:],
+                )
 
         banks = {}
         grouped = {}
@@ -175,20 +191,24 @@ def tile_selfattention_pa_kernel(tc, x, W, b, out_0, out_1, out_2):
                             a == 0, srt[:, :, w0 // 2:w0 // 2 + 256], w32[:, w0:w0 + 512]
                         )
             else:
-                sort_words(True, srt[:], w32)
+                n = SV if is_v(k) else SQK
+                sort_words(True, srt[:, :, 0:1024 - n], w32[:, 0:2048 - 2 * n])
+                if n:
+                    sort_words(False, srt[:, :, 1024 - n:1024], w32[:, 2048 - 2 * n:2048])
             sorted_words[k] = srt
 
-        def stage_t(k):
+        def stage_t(k, half):
             srt = sorted_words[k]
-            for g in range(4):
+            for g in (2 * half, 2 * half + 1):
                 banks[(k, g)] = transposes_into_bank(
                     [
                         srt[:, u, 512 * a + P * g:512 * a + P * (g + 1)]
                         for a in range(2) for u in range(2)
                     ]
                 )
-            if k + W_AHEAD < NSLOT:
-                load_w(k + W_AHEAD, 1)
+            nxt_w = k + W_AHEAD - 1
+            if half == 1 and nxt_w < NSLOT:
+                load_w(nxt_w, 1)
 
         def stage_d(k, g, on_vector):
             grp = gpool.tile([P, 1024], BF16, name="grp", align_bytes=64)
@@ -209,9 +229,10 @@ def tile_selfattention_pa_kernel(tc, x, W, b, out_0, out_1, out_2):
             )
             codes[(k, g)] = (cd, sc)
 
-        def stage_m(k):
-            acc[k] = opsum.tile([P, 512], F32, name="acc")
-            for m in range(2):
+        def stage_m(k, ms=(0, 1)):
+            if ms[0] == 0:
+                acc[k] = opsum.tile([P, 512], F32, name="acc")
+            for m in ms:
                 for g in range(4):
                     cd, sc = codes[(k, g)]
                     xcol = (4 * m + g) * P
@@ -225,18 +246,27 @@ def tile_selfattention_pa_kernel(tc, x, W, b, out_0, out_1, out_2):
                         stop=(g == 3),
                     )
 
-        def y_part(k):
+        def y_tile(k):
             h = first_head(k)
-            y = ytile[h // HSB]
-            hl = h % HSB
+            key = (is_v(k), h // HSB)
+            if key not in ytile:
+                if is_v(k):
+                    yv = ypool.tile([P, 2, 1, HSB, HD], F32, name="yv")
+                    ytile[key] = yv
+                else:
+                    yqk = ypool.tile([P, 2, 2, HSB, HD], F32, name="yqk")
+                    ytile[key] = yqk
+            return ytile[key]
+
+        def y_part(k):
+            y = y_tile(k)
+            hl = first_head(k) % HSB
             if is_v(k):
-                return y[:, :, 2, hl:hl + 2, :]
-            return y[:, :, 0:2, hl, :]
+                return y[:, :, 0, hl:hl + 2, :]
+            return y[:, :, :, hl, :]
 
         def stage_a(k):
             h = first_head(k)
-            if h % HSB == 0 and not is_v(k):
-                ytile[h // HSB] = ypool.tile([P, 2, 3, HSB, HD], F32, name="y")
             if is_v(k):
                 bias = bias_bc[:, 384 * h:384 * h + 768].rearrange(
                     "q (g s c) -> q s g c", g=2, s=3
@@ -252,7 +282,7 @@ def tile_selfattention_pa_kernel(tc, x, W, b, out_0, out_1, out_2):
 
         def norm_ap(k, j):
             h = first_head(k)
-            return ytile[h // HSB][:, j // 2, j % 2, h % HSB, :]
+            return y_tile(k)[:, j // 2, j % 2, h % HSB, :]
 
         def stage_sq(k, j):
             if j == 0:
@@ -279,19 +309,25 @@ def tile_selfattention_pa_kernel(tc, x, W, b, out_0, out_1, out_2):
         def stage_scale(k):
             rn = stats[(k, "rn")]
             for j in range(4):
+                if j >= 4 - CS:
+                    nc.scalar.activation(
+                        out=norm_ap(k, j), in_=norm_ap(k, j), func=ACT.Copy,
+                        scale=rn[:, j:j + 1],
+                    )
+                    continue
                 nc.vector.tensor_scalar(
                     out=norm_ap(k, j), in0=norm_ap(k, j), scalar1=rn[:, j:j + 1],
                     scalar2=None, op0=ALU.mult,
                 )
 
         def store(s, h0, n):
-            y = ytile[h0 // HSB]
+            y = ytile[(s == 2, h0 // HSB)]
             hl = h0 % HSB
             for m in range(2):
                 for bl in range(2):
                     nc.sync.dma_start(
                         out=outs[s][2 * m + bl, h0:h0 + n, :, :].rearrange("h l c -> l h c"),
-                        in_=y[bl:P:2, m, s, hl:hl + n, :],
+                        in_=y[bl:P:2, m, s % 2, hl:hl + n, :],
                     )
 
         def active(k):
@@ -329,32 +365,44 @@ def tile_selfattention_pa_kernel(tc, x, W, b, out_0, out_1, out_2):
 
         stage_p(0)
         for k in range(NSLOT):
-            stage_t(k)
-            if k == 0:
-                for m in range(2):
-                    sort_words(m == 1, xsort[m][:], x_sb[m][:].bitcast(F32))
+            stage_t(k, 0)
+            if SPLIT and k >= 2:
+                stage_m(k - 2, (0,))
+            stage_t(k, 1)
             if k == 0:
                 stage_d(k, 0, False)
-                stage_d(k, 1, True)
+                stage_d(k, 1, DV)
                 stage_d(k, 2, False)
-                stage_d(k, 3, True)
-                if not BIASDMA:
-                    bias_pair(2, True)
-                    bias_pair(3, True)
+                stage_d(k, 3, DV)
+                xsort = ppool.tile([P, 2, 1024], F32, name="srt")
+                x32 = x_sb[:].rearrange("p m k -> p (m k)").bitcast(F32)
+                for m in range(2):
+                    sort_words(
+                        m == 1, xsort[:, :, 512 * m:512 * (m + 1)],
+                        x32[:, 1024 * m:1024 * (m + 1)],
+                    )
+                for g in range(4):
+                    stage_q(0, g)
+                bias_pair(2, False)
+                bias_pair(3, False)
+                stage_p(1)
                 stage_x(0, False)
-                stage_x(1, True)
+                stage_x(1, XV)
             for c in VORD:
                 if c == "A":
                     run("A", k - LA, do_a)
                 if c == "C":
                     run("C", k - LC, do_c)
                 if c == "P":
-                    if k + 1 < NSLOT:
-                        stage_p(k + 1)
-                    if k == 1:
+                    if k == 1 and XQ1:
                         stage_xq(0)
                         stage_xq(1)
-                if c == "Q" and k > 0:
+                    if 0 < k < NSLOT - 1:
+                        stage_p(k + 1)
+                    if k == 1 and not XQ1:
+                        stage_xq(0)
+                        stage_xq(1)
+                if c == "Q" and k > 1:
                     for g in range(4):
                         stage_q(k - 1, g)
             nd = 0
@@ -378,9 +426,10 @@ def tile_selfattention_pa_kernel(tc, x, W, b, out_0, out_1, out_2):
             if k in (1, 2) and not BIASDMA:
                 bias_pair(2 * k + 2, BV)
                 bias_pair(2 * k + 3, BV)
-            if k % RUN == RUN - 1:
-                run("M", k - 2, stage_m)
+            if k >= 2:
+                stage_m(k - 2, (1,) if SPLIT else (0, 1))
 
+        nxt["M"] = NSLOT - 2
         last = NSLOT - 1
         for g in range(4):
             stage_q(last, g)

@@ -25,19 +25,25 @@ BV = False
 LA = 3
 LSQ = 3
 LX = 4
-LC = 5
+LC = 4
 RUN = 1
 XQ1 = False
+QP0 = 1
+QP = 1
+QPL = 4
+CB = 3
 YB = 4
-SV = 0
+SV = 256
+SVK = 20
+CSO = 1
 SQK = 0
-SPLIT = True
+SPLIT = False
 CS = 1
 DV = True
 XV = True
-VORD = "PACQ"
+VORD = "PAQ"
 SORD = "000r101"
-FINE = 2
+FINE = 4
 FINEV = 4
 BIASDMA = 0
 GT = 0
@@ -51,8 +57,8 @@ def tile_selfattention_pa_kernel(tc, x, W, b, out_0, out_1, out_2):
         const = ctx.enter_context(tc.tile_pool(name="const", bufs=1))
         wpool = ctx.enter_context(tc.tile_pool(name="wpool", bufs=W_AHEAD))
         ppool = ctx.enter_context(tc.tile_pool(name="ppool", bufs=3))
-        gpool = ctx.enter_context(tc.tile_pool(name="gpool", bufs=12))
-        cpool = ctx.enter_context(tc.tile_pool(name="cpool", bufs=12))
+        gpool = ctx.enter_context(tc.tile_pool(name="gpool", bufs=3))
+        cpool = ctx.enter_context(tc.tile_pool(name="cpool", bufs=CB))
         ypool = ctx.enter_context(tc.tile_pool(name="ypool", bufs=YB))
         spool = ctx.enter_context(tc.tile_pool(name="spool", bufs=4))
         tpsum = ctx.enter_context(tc.psum_pool(name="tpsum", bufs=T_BANKS))
@@ -150,22 +156,23 @@ def tile_selfattention_pa_kernel(tc, x, W, b, out_0, out_1, out_2):
                         for g in (2 * gp, 2 * gp + 1) for u in range(2)
                     ]
                 )
-                grp = gpool.tile([P, 1024], BF16, name="grp", align_bytes=64)
-                xgrp[(m, gp)] = grp
+                if m == 0 and gp == 0:
+                    xgrp[0] = gpool.tile([P, 4096], BF16, name="grp", align_bytes=64)
+                w0 = 1024 * m + 512 * gp
                 drain(
                     on_vector,
-                    grp[:].bitcast(F32).rearrange("q (a c u) -> q a c u", a=2, u=2),
+                    xgrp[0][:].bitcast(F32)[:, w0:w0 + 512].rearrange(
+                        "q (a c u) -> q a c u", a=2, u=2
+                    ),
                     tb[:].rearrange("q (a u c) -> q a c u", a=2, u=2),
                 )
 
         def stage_xq(m):
-            for gp in range(2):
-                c0 = 512 * m + 256 * gp
-                nc.vector.quantize_mx(
-                    out=xc[:, c0:c0 + 256].bitcast(FP8X4),
-                    scales=xs[:, c0:c0 + 256],
-                    in_=xgrp[(m, gp)][:],
-                )
+            nc.vector.quantize_mx(
+                out=xc[:, 512 * m:512 * (m + 1)].bitcast(FP8X4),
+                scales=xs[:, 512 * m:512 * (m + 1)],
+                in_=xgrp[0][:, 2048 * m:2048 * (m + 1)],
+            )
 
         banks = {}
         grouped = {}
@@ -191,7 +198,7 @@ def tile_selfattention_pa_kernel(tc, x, W, b, out_0, out_1, out_2):
                             a == 0, srt[:, :, w0 // 2:w0 // 2 + 256], w32[:, w0:w0 + 512]
                         )
             else:
-                n = SV if is_v(k) else SQK
+                n = SV if k >= SVK else SQK
                 sort_words(True, srt[:, :, 0:1024 - n], w32[:, 0:2048 - 2 * n])
                 if n:
                     sort_words(False, srt[:, :, 1024 - n:1024], w32[:, 2048 - 2 * n:2048])
@@ -211,37 +218,41 @@ def tile_selfattention_pa_kernel(tc, x, W, b, out_0, out_1, out_2):
                 load_w(nxt_w, 1)
 
         def stage_d(k, g, on_vector):
-            grp = gpool.tile([P, 1024], BF16, name="grp", align_bytes=64)
-            grouped[(k, g)] = grp
+            if g == 0:
+                grouped[k] = gpool.tile([P, 4096], BF16, name="grp", align_bytes=64)
             src = banks[(k, g)][:]
-            dst = grp[:].bitcast(F32)
+            dst = grouped[k][:].bitcast(F32)[:, 512 * g:512 * (g + 1)]
             drain(
                 on_vector,
                 dst.rearrange("q (a c u) -> q a c u", a=2, u=2),
                 src.rearrange("q (a u c) -> q a c u", a=2, u=2),
             )
 
-        def stage_q(k, g):
-            cd = cpool.tile([P, 256], U32, name="cd", align_bytes=64)
-            sc = cpool.tile([P, 256], U8, name="sc", align_bytes=64)
-            nc.vector.quantize_mx(
-                out=cd[:].bitcast(FP8X4), scales=sc[:], in_=grouped[(k, g)][:]
-            )
-            codes[(k, g)] = (cd, sc)
+        def stage_q(k, pieces):
+            cd = cpool.tile([P, 1024], U32, name="cd", align_bytes=64)
+            sc = cpool.tile([P, 1024], U8, name="sc", align_bytes=64)
+            n = 1024 // pieces
+            for j in range(pieces):
+                nc.vector.quantize_mx(
+                    out=cd[:, n * j:n * (j + 1)].bitcast(FP8X4),
+                    scales=sc[:, n * j:n * (j + 1)],
+                    in_=grouped[k][:, 4 * n * j:4 * n * (j + 1)],
+                )
+            codes[k] = (cd, sc)
 
         def stage_m(k, ms=(0, 1)):
             if ms[0] == 0:
                 acc[k] = opsum.tile([P, 512], F32, name="acc")
             for m in ms:
                 for g in range(4):
-                    cd, sc = codes[(k, g)]
+                    cd, sc = codes[k]
                     xcol = (4 * m + g) * P
                     nc.tensor.matmul_mx(
                         out=acc[k][:, 256 * m:256 * (m + 1)],
                         lhsT=xc[:, xcol:xcol + P].bitcast(FP8X4),
                         lhsT_scale=xs[:, xcol:xcol + P],
-                        rhs=cd[:].bitcast(FP8X4),
-                        rhs_scale=sc[:],
+                        rhs=cd[:, 256 * g:256 * (g + 1)].bitcast(FP8X4),
+                        rhs_scale=sc[:, 256 * g:256 * (g + 1)],
                         start=(g == 0),
                         stop=(g == 3),
                     )
@@ -309,7 +320,7 @@ def tile_selfattention_pa_kernel(tc, x, W, b, out_0, out_1, out_2):
         def stage_scale(k):
             rn = stats[(k, "rn")]
             for j in range(4):
-                if j >= 4 - CS:
+                if j >= 4 - (CSO if first_head(k) % 2 else CS):
                     nc.scalar.activation(
                         out=norm_ap(k, j), in_=norm_ap(k, j), func=ACT.Copy,
                         scale=rn[:, j:j + 1],
@@ -381,8 +392,7 @@ def tile_selfattention_pa_kernel(tc, x, W, b, out_0, out_1, out_2):
                         m == 1, xsort[:, :, 512 * m:512 * (m + 1)],
                         x32[:, 1024 * m:1024 * (m + 1)],
                     )
-                for g in range(4):
-                    stage_q(0, g)
+                stage_q(0, QP0)
                 bias_pair(2, False)
                 bias_pair(3, False)
                 stage_p(1)
@@ -391,8 +401,6 @@ def tile_selfattention_pa_kernel(tc, x, W, b, out_0, out_1, out_2):
             for c in VORD:
                 if c == "A":
                     run("A", k - LA, do_a)
-                if c == "C":
-                    run("C", k - LC, do_c)
                 if c == "P":
                     if k == 1 and XQ1:
                         stage_xq(0)
@@ -403,8 +411,7 @@ def tile_selfattention_pa_kernel(tc, x, W, b, out_0, out_1, out_2):
                         stage_xq(0)
                         stage_xq(1)
                 if c == "Q" and k > 1:
-                    for g in range(4):
-                        stage_q(k - 1, g)
+                    stage_q(k - 1, QP)
             nd = 0
             sqs = []
             run("S", k - LSQ, sqs.append)
@@ -423,6 +430,7 @@ def tile_selfattention_pa_kernel(tc, x, W, b, out_0, out_1, out_2):
                     run("r", k - LX, stage_rsqrt)
             for j, i in pieces:
                 stage_sq(j, i)
+            run("C", k - LC, do_c)
             if k in (1, 2) and not BIASDMA:
                 bias_pair(2 * k + 2, BV)
                 bias_pair(2 * k + 3, BV)
@@ -431,8 +439,7 @@ def tile_selfattention_pa_kernel(tc, x, W, b, out_0, out_1, out_2):
 
         nxt["M"] = NSLOT - 2
         last = NSLOT - 1
-        for g in range(4):
-            stage_q(last, g)
+        stage_q(last, QPL)
         run("M", last, stage_m)
 
         def square_all(j):

@@ -34,17 +34,22 @@ QPL = 4
 CB = 3
 YB = 4
 SV = 256
-SVK = 20
+SVK = 21
+SVE = 23
+QP22 = 2
+LASTM = 23
+VF = 8
+FINL = 4
 CSO = 1
 SQK = 0
 SPLIT = False
-CS = 1
+CS = 0
 DV = True
 XV = True
 VORD = "PAQ"
-SORD = "000r101"
+SORD = "00r0011"
 FINE = 4
-FINEV = 4
+FINEV = 2
 BIASDMA = 0
 GT = 0
 FLOPS = 2 * 256 * 2048 * 6144
@@ -198,7 +203,7 @@ def tile_selfattention_pa_kernel(tc, x, W, b, out_0, out_1, out_2):
                             a == 0, srt[:, :, w0 // 2:w0 // 2 + 256], w32[:, w0:w0 + 512]
                         )
             else:
-                n = SV if k >= SVK else SQK
+                n = SV if SVK <= k < SVE else SQK
                 sort_words(True, srt[:, :, 0:1024 - n], w32[:, 0:2048 - 2 * n])
                 if n:
                     sort_words(False, srt[:, :, 1024 - n:1024], w32[:, 2048 - 2 * n:2048])
@@ -241,14 +246,16 @@ def tile_selfattention_pa_kernel(tc, x, W, b, out_0, out_1, out_2):
             codes[k] = (cd, sc)
 
         def stage_m(k, ms=(0, 1)):
-            if ms[0] == 0:
-                acc[k] = opsum.tile([P, 512], F32, name="acc")
             for m in ms:
+                if m == 0 or k == LASTM:
+                    acc[(k, m)] = opsum.tile([P, 512], F32, name="acc")
+                else:
+                    acc[(k, 1)] = acc[(k, 0)]
                 for g in range(4):
                     cd, sc = codes[k]
                     xcol = (4 * m + g) * P
                     nc.tensor.matmul_mx(
-                        out=acc[k][:, 256 * m:256 * (m + 1)],
+                        out=acc[(k, m)][:, 256 * m:256 * (m + 1)],
                         lhsT=xc[:, xcol:xcol + P].bitcast(FP8X4),
                         lhsT_scale=xs[:, xcol:xcol + P],
                         rhs=cd[:, 256 * g:256 * (g + 1)].bitcast(FP8X4),
@@ -276,7 +283,7 @@ def tile_selfattention_pa_kernel(tc, x, W, b, out_0, out_1, out_2):
                 return y[:, :, 0, hl:hl + 2, :]
             return y[:, :, :, hl, :]
 
-        def stage_a(k):
+        def stage_a(k, m0=0, m1=2):
             h = first_head(k)
             if is_v(k):
                 bias = bias_bc[:, 384 * h:384 * h + 768].rearrange(
@@ -285,9 +292,9 @@ def tile_selfattention_pa_kernel(tc, x, W, b, out_0, out_1, out_2):
             else:
                 bias = bias_bc[:, 384 * h:384 * h + 256].rearrange("q (g c) -> q g c", g=2)
             nc.vector.tensor_tensor(
-                out=y_part(k),
-                in0=acc[k][:].rearrange("q (m g c) -> q m g c", m=2, g=2),
-                in1=bias.unsqueeze(1).to_broadcast([P, 2, 2, HD]),
+                out=y_part(k)[:, m0:m1],
+                in0=acc[(k, m0)][:].rearrange("q (m g c) -> q m g c", m=2, g=2)[:, m0:m1],
+                in1=bias.unsqueeze(1).to_broadcast([P, m1 - m0, 2, HD]),
                 op=ALU.add,
             )
 
@@ -331,10 +338,10 @@ def tile_selfattention_pa_kernel(tc, x, W, b, out_0, out_1, out_2):
                     scalar2=None, op0=ALU.mult,
                 )
 
-        def store(s, h0, n):
+        def store(s, h0, n, ms=(0, 1)):
             y = ytile[(s == 2, h0 // HSB)]
             hl = h0 % HSB
-            for m in range(2):
+            for m in ms:
                 for bl in range(2):
                     nc.sync.dma_start(
                         out=outs[s][2 * m + bl, h0:h0 + n, :, :].rearrange("h l c -> l h c"),
@@ -360,10 +367,15 @@ def tile_selfattention_pa_kernel(tc, x, W, b, out_0, out_1, out_2):
                     fn(j)
 
         def do_a(j):
+            if j == LASTM:
+                for m in range(2):
+                    stage_a(j, m, m + 1)
+                    store(2, NH - FINL, FINL, (m,))
+                return
             stage_a(j)
             h = first_head(j)
-            n = HSB if h < NH - HSB else FINEV
-            if is_v(j) and (h + 2) % n == 0:
+            n = HSB if h < NH - VF else FINEV
+            if is_v(j) and (h + 2) % n == 0 and (h < NH - FINL):
                 store(2, h + 2 - n, n)
 
         def do_c(j):
@@ -411,7 +423,7 @@ def tile_selfattention_pa_kernel(tc, x, W, b, out_0, out_1, out_2):
                         stage_xq(0)
                         stage_xq(1)
                 if c == "Q" and k > 1:
-                    stage_q(k - 1, QP)
+                    stage_q(k - 1, QP if k < NSLOT - 1 else QP22)
             nd = 0
             sqs = []
             run("S", k - LSQ, sqs.append)

@@ -25,7 +25,7 @@ BV = False
 LA = 3
 LSQ = 3
 LX = 4
-LC = 4
+LC = 5
 RUN = 1
 XQ1 = False
 QP0 = 1
@@ -43,11 +43,11 @@ FINL = 4
 CSO = 1
 SQK = 0
 SPLIT = False
-CS = 0
+CS = 1
 DV = True
 XV = True
-VORD = "PAQ"
-SORD = "00r0011"
+VORD = "PXAQ"
+SORD = "000r011"
 FINE = 4
 FINEV = 2
 BIASDMA = 0
@@ -313,7 +313,7 @@ def tile_selfattention_pa_kernel(tc, x, W, b, out_0, out_1, out_2):
 
         def stage_max(k):
             stats[(k, "sc")] = spool.tile([P, 4], F32, name="ssc")
-            nc.gpsimd.tensor_scalar_max(
+            nc.vector.tensor_scalar_max(
                 out=stats[(k, "sc")][:], in0=stats[(k, "ss")][:], scalar1=1e-24
             )
 
@@ -413,6 +413,8 @@ def tile_selfattention_pa_kernel(tc, x, W, b, out_0, out_1, out_2):
             for c in VORD:
                 if c == "A":
                     run("A", k - LA, do_a)
+                if c == "X":
+                    run("X", k - LX, stage_max)
                 if c == "P":
                     if k == 1 and XQ1:
                         stage_xq(0)
@@ -438,7 +440,6 @@ def tile_selfattention_pa_kernel(tc, x, W, b, out_0, out_1, out_2):
                         stage_sq(j, i)
                     pieces = pieces[2:]
                 if c == "r":
-                    run("X", k - LX, stage_max)
                     run("r", k - LX, stage_rsqrt)
             for j, i in pieces:
                 stage_sq(j, i)

from contextlib import ExitStack

import concourse.mybir as mybir
from concourse.masks import make_identity

F32 = mybir.dt.float32
BF16 = mybir.dt.bfloat16
U32 = mybir.dt.uint32
U8 = mybir.dt.uint8
I32 = mybir.dt.int32
FP8X4 = mybir.dt.float8_e4m3fn_x4
ALU = mybir.AluOpType
ACT = mybir.ActivationFunctionType

P = 128
E = 2048
NH = 16
HD = 128
NSLOT = 24
W_AHEAD = 12
T_BANKS = 5
HSB = 4
QKG = (16,)
BV = False
LA = 3
LSQ = 3
LX = 4
LC = 5
RUN = 1
XQ1 = False
QP0 = 1
QP = 1
QPL = 4
CB = 3
YB = 4
SV = 256
SVK = 21
SVE = 23
QP22 = 2
LASTM = 23
VF = 8
FINL = 4
CSO = 1
SQK = 0
SPLIT = False
CS = 1
DV = True
XV = True
VORD = "PXAQ"
SORD = "000r011"
FINE = 4
FINEV = 2
BIASDMA = 0
GT = 0
FLOPS = 2 * 256 * 2048 * 6144


def tile_selfattention_pa_kernel(tc, x, W, b, out_0, out_1, out_2):
    nc = tc.nc
    outs = (out_0, out_1, out_2)
    with ExitStack() as ctx:
        const = ctx.enter_context(tc.tile_pool(name="const", bufs=1))
        wpool = ctx.enter_context(tc.tile_pool(name="wpool", bufs=W_AHEAD))
        ppool = ctx.enter_context(tc.tile_pool(name="ppool", bufs=3))
        gpool = ctx.enter_context(tc.tile_pool(name="gpool", bufs=3))
        cpool = ctx.enter_context(tc.tile_pool(name="cpool", bufs=CB))
        ypool = ctx.enter_context(tc.tile_pool(name="ypool", bufs=YB))
        spool = ctx.enter_context(tc.tile_pool(name="spool", bufs=4))
        tpsum = ctx.enter_context(tc.psum_pool(name="tpsum", bufs=T_BANKS))
        opsum = ctx.enter_context(tc.psum_pool(name="opsum", bufs=8 - T_BANKS))
        ctx.enter_context(tc.manual_schedule())

        ident_f = const.tile([P, P], F32, name="ident_f")
        ident_b = const.tile([P, P], BF16, name="ident_b")
        b_sb = const.tile([P, 384], BF16, name="b_sb")
        bias_bc = const.tile([P, 6144], BF16, name="bias_bc")
        warm = const.tile([P, 1], F32, name="warm")
        warm2 = const.tile([P, 1], F32, name="warm2")
        xc = const.tile([P, 1024], U32, name="xc", align_bytes=64)
        xs = const.tile([P, 1024], U8, name="xs", align_bytes=64)

        slots = []
        h0 = 0
        for n in QKG:
            slots += [(h, False) for h in range(h0, h0 + n)]
            slots += [(h, True) for h in range(h0, h0 + n, 2)]
            h0 += n

        def is_v(k):
            return slots[k][1]

        def first_head(k):
            return slots[k][0]

        w_tiles = {}

        def w_rows(k):
            r0 = 384 * first_head(k)
            if is_v(k):
                return W[r0:r0 + 768, :].rearrange("(t r p) k -> r p t k", t=2, r=3)[2]
            return W[r0:r0 + 256, :].rearrange("(t p) k -> p t k", t=2)

        def load_w(k, pieces):
            w_sb = wpool.tile([P, 2, E], BF16, name="w_sb")
            rows = w_rows(k)
            n = E // pieces
            for j in range(pieces):
                nc.sync.dma_start(
                    out=w_sb[:, :, n * j:n * (j + 1)], in_=rows[:, :, n * j:n * (j + 1)]
                )
            w_tiles[k] = w_sb

        nc.vector.memset(b_sb[:].bitcast(I32), 0)
        nc.vector.memset(warm[:], 1.0)
        nc.sync.dma_start(out=b_sb[0:16, :], in_=b.rearrange("(h n) -> h n", h=16))
        load_w(0, 2)
        x_sb = wpool.tile([P, 2, E], BF16, name="w_sb")
        for m in range(2):
            for bl in range(2):
                nc.sync.dma_start(out=x_sb[bl:P:2, m, :], in_=x[2 * m + bl, :, :])
        for k in range(1, W_AHEAD - 1):
            load_w(k, 1)
        make_identity(nc, ident_b[:])
        make_identity(nc, ident_f[:])
        nc.scalar.activation(out=warm2[:], in_=warm[:], func=ACT.Abs_reciprocal_sqrt)

        def drain(on_vector, dst, src):
            if on_vector:
                nc.vector.tensor_copy(out=dst, in_=src)
            else:
                nc.scalar.copy(out=dst, in_=src)

        def bias_pair(j, on_vector):
            tb = tpsum.tile([P, 1024], BF16, name="tb")
            for h in (2 * j, 2 * j + 1):
                c0 = 384 * (h - 2 * j)
                nc.tensor.matmul(
                    out=tb[:, c0:c0 + 384],
                    lhsT=ident_b[:, h:h + 1].to_broadcast([P, P]),
                    rhs=b_sb[:],
                    start=True,
                    stop=True,
                )
            drain(on_vector, bias_bc[:, 768 * j:768 * (j + 1)], tb[:, 0:768])

        def transposes_into_bank(operands):
            tb = tpsum.tile([P, 512], F32, name="tb")
            for j, op in enumerate(operands):
                nc.tensor.transpose(
                    out=tb[:, j * P:(j + 1) * P], in_=op, identity=ident_f[:]
                )
            return tb

        xgrp = {}

        def stage_x(m, on_vector):
            for gp in range(2):
                tb = transposes_into_bank(
                    [
                        xsort[:, u, 512 * m + P * g:512 * m + P * (g + 1)]
                        for g in (2 * gp, 2 * gp + 1) for u in range(2)
                    ]
                )
                if m == 0 and gp == 0:
                    xgrp[0] = gpool.tile([P, 4096], BF16, name="grp", align_bytes=64)
                w0 = 1024 * m + 512 * gp
                drain(
                    on_vector,
                    xgrp[0][:].bitcast(F32)[:, w0:w0 + 512].rearrange(
                        "q (a c u) -> q a c u", a=2, u=2
                    ),
                    tb[:].rearrange("q (a u c) -> q a c u", a=2, u=2),
                )

        def stage_xq(m):
            nc.vector.quantize_mx(
                out=xc[:, 512 * m:512 * (m + 1)].bitcast(FP8X4),
                scales=xs[:, 512 * m:512 * (m + 1)],
                in_=xgrp[0][:, 2048 * m:2048 * (m + 1)],
            )

        banks = {}
        grouped = {}
        codes = {}
        acc = {}
        ytile = {}
        stats = {}
        sorted_words = {}

        def sort_words(eng_v, dst, src):
            d = dst.rearrange("p u (j i) -> p u j i", i=8)
            s = src.rearrange("p (j u i) -> p u j i", u=2, i=8)
            drain(eng_v, d, s)

        def stage_p(k):
            srt = ppool.tile([P, 2, 1024], F32, name="srt")
            w32 = w_tiles[k][:].rearrange("p t k -> p (t k)").bitcast(F32)
            if k == 0:
                for a in range(2):
                    for h in range(2):
                        w0 = 1024 * a + 512 * h
                        sort_words(
                            a == 0, srt[:, :, w0 // 2:w0 // 2 + 256], w32[:, w0:w0 + 512]
                        )
            else:
                n = SV if SVK <= k < SVE else SQK
                sort_words(True, srt[:, :, 0:1024 - n], w32[:, 0:2048 - 2 * n])
                if n:
                    sort_words(False, srt[:, :, 1024 - n:1024], w32[:, 2048 - 2 * n:2048])
            sorted_words[k] = srt

        def stage_t(k, half):
            srt = sorted_words[k]
            for g in (2 * half, 2 * half + 1):
                banks[(k, g)] = transposes_into_bank(
                    [
                        srt[:, u, 512 * a + P * g:512 * a + P * (g + 1)]
                        for a in range(2) for u in range(2)
                    ]
                )
            nxt_w = k + W_AHEAD - 1
            if half == 1 and nxt_w < NSLOT:
                load_w(nxt_w, 1)

        def stage_d(k, g, on_vector):
            if g == 0:
                grouped[k] = gpool.tile([P, 4096], BF16, name="grp", align_bytes=64)
            src = banks[(k, g)][:]
            dst = grouped[k][:].bitcast(F32)[:, 512 * g:512 * (g + 1)]
            drain(
                on_vector,
                dst.rearrange("q (a c u) -> q a c u", a=2, u=2),
                src.rearrange("q (a u c) -> q a c u", a=2, u=2),
            )

        def stage_q(k, pieces):
            cd = cpool.tile([P, 1024], U32, name="cd", align_bytes=64)
            sc = cpool.tile([P, 1024], U8, name="sc", align_bytes=64)
            n = 1024 // pieces
            for j in range(pieces):
                nc.vector.quantize_mx(
                    out=cd[:, n * j:n * (j + 1)].bitcast(FP8X4),
                    scales=sc[:, n * j:n * (j + 1)],
                    in_=grouped[k][:, 4 * n * j:4 * n * (j + 1)],
                )
            codes[k] = (cd, sc)

        def stage_m(k, ms=(0, 1)):
            for m in ms:
                if m == 0 or k == LASTM:
                    acc[(k, m)] = opsum.tile([P, 512], F32, name="acc")
                else:
                    acc[(k, 1)] = acc[(k, 0)]
                for g in range(4):
                    cd, sc = codes[k]
                    xcol = (4 * m + g) * P
                    nc.tensor.matmul_mx(
                        out=acc[(k, m)][:, 256 * m:256 * (m + 1)],
                        lhsT=xc[:, xcol:xcol + P].bitcast(FP8X4),
                        lhsT_scale=xs[:, xcol:xcol + P],
                        rhs=cd[:, 256 * g:256 * (g + 1)].bitcast(FP8X4),
                        rhs_scale=sc[:, 256 * g:256 * (g + 1)],
                        start=(g == 0),
                        stop=(g == 3),
                    )

        def y_tile(k):
            h = first_head(k)
            key = (is_v(k), h // HSB)
            if key not in ytile:
                if is_v(k):
                    yv = ypool.tile([P, 2, 1, HSB, HD], F32, name="yv")
                    ytile[key] = yv
                else:
                    yqk = ypool.tile([P, 2, 2, HSB, HD], F32, name="yqk")
                    ytile[key] = yqk
            return ytile[key]

        def y_part(k):
            y = y_tile(k)
            hl = first_head(k) % HSB
            if is_v(k):
                return y[:, :, 0, hl:hl + 2, :]
            return y[:, :, :, hl, :]

        def stage_a(k, m0=0, m1=2):
            h = first_head(k)
            if is_v(k):
                bias = bias_bc[:, 384 * h:384 * h + 768].rearrange(
                    "q (g s c) -> q s g c", g=2, s=3
                )[:, 2]
            else:
                bias = bias_bc[:, 384 * h:384 * h + 256].rearrange("q (g c) -> q g c", g=2)
            nc.vector.tensor_tensor(
                out=y_part(k)[:, m0:m1],
                in0=acc[(k, m0)][:].rearrange("q (m g c) -> q m g c", m=2, g=2)[:, m0:m1],
                in1=bias.unsqueeze(1).to_broadcast([P, m1 - m0, 2, HD]),
                op=ALU.add,
            )

        def norm_ap(k, j):
            h = first_head(k)
            return y_tile(k)[:, j // 2, j % 2, h % HSB, :]

        def stage_sq(k, j):
            if j == 0:
                stats[(k, "ss")] = spool.tile([P, 4], F32, name="ss")
            sq = spool.tile([P, P], F32, name="sq")
            nc.scalar.activation(
                out=sq[:], in_=norm_ap(k, j), func=ACT.Square,
                accum_out=stats[(k, "ss")][:, j:j + 1],
            )

        def stage_max(k):
            stats[(k, "sc")] = spool.tile([P, 4], F32, name="ssc")
            nc.vector.tensor_scalar_max(
                out=stats[(k, "sc")][:], in0=stats[(k, "ss")][:], scalar1=1e-24
            )

        def stage_rsqrt(k):
            stats[(k, "rn")] = spool.tile([P, 4], F32, name="rn")
            nc.scalar.activation(
                out=stats[(k, "rn")][:], in_=stats[(k, "sc")][:],
                func=ACT.Abs_reciprocal_sqrt,
            )

        def stage_scale(k):
            rn = stats[(k, "rn")]
            for j in range(4):
                if j >= 4 - (CSO if first_head(k) % 2 else CS):
                    nc.scalar.activation(
                        out=norm_ap(k, j), in_=norm_ap(k, j), func=ACT.Copy,
                        scale=rn[:, j:j + 1],
                    )
                    continue
                nc.vector.tensor_scalar(
                    out=norm_ap(k, j), in0=norm_ap(k, j), scalar1=rn[:, j:j + 1],
                    scalar2=None, op0=ALU.mult,
                )

        def store(s, h0, n, ms=(0, 1)):
            y = ytile[(s == 2, h0 // HSB)]
            hl = h0 % HSB
            for m in ms:
                for bl in range(2):
                    nc.sync.dma_start(
                        out=outs[s][2 * m + bl, h0:h0 + n, :, :].rearrange("h l c -> l h c"),
                        in_=y[bl:P:2, m, s % 2, hl:hl + n, :],
                    )

        def active(k):
            return 0 <= k < NSLOT

        def active_qk(k):
            return active(k) and not is_v(k)

        if not BIASDMA:
            bias_pair(0, True)
            bias_pair(1, False)
        nxt = {"A": 0, "S": 0, "X": 0, "r": 0, "R": 0, "C": 0, "M": 0}

        def run(stage, last, fn):
            while nxt[stage] <= min(last, NSLOT - 1):
                j = nxt[stage]
                nxt[stage] = j + 1
                if stage in ("A", "M") or not is_v(j):
                    fn(j)

        def do_a(j):
            if j == LASTM:
                for m in range(2):
                    stage_a(j, m, m + 1)
                    store(2, NH - FINL, FINL, (m,))
                return
            stage_a(j)
            h = first_head(j)
            n = HSB if h < NH - VF else FINEV
            if is_v(j) and (h + 2) % n == 0 and (h < NH - FINL):
                store(2, h + 2 - n, n)

        def do_c(j):
            stage_scale(j)
            h = first_head(j)
            n = HSB if h < NH - HSB else FINE
            if (h + 1) % n == 0:
                store(0, h + 1 - n, n)
                store(1, h + 1 - n, n)

        stage_p(0)
        for k in range(NSLOT):
            stage_t(k, 0)
            if SPLIT and k >= 2:
                stage_m(k - 2, (0,))
            stage_t(k, 1)
            if k == 0:
                stage_d(k, 0, False)
                stage_d(k, 1, DV)
                stage_d(k, 2, False)
                stage_d(k, 3, DV)
                xsort = ppool.tile([P, 2, 1024], F32, name="srt")
                x32 = x_sb[:].rearrange("p m k -> p (m k)").bitcast(F32)
                for m in range(2):
                    sort_words(
                        m == 1, xsort[:, :, 512 * m:512 * (m + 1)],
                        x32[:, 1024 * m:1024 * (m + 1)],
                    )
                stage_q(0, QP0)
                bias_pair(2, False)
                bias_pair(3, False)
                stage_p(1)
                stage_x(0, False)
                stage_x(1, XV)
            for c in VORD:
                if c == "A":
                    run("A", k - LA, do_a)
                if c == "X":
                    run("X", k - LX, stage_max)
                if c == "P":
                    if k == 1 and XQ1:
                        stage_xq(0)
                        stage_xq(1)
                    if 0 < k < NSLOT - 1:
                        stage_p(k + 1)
                    if k == 1 and not XQ1:
                        stage_xq(0)
                        stage_xq(1)
                if c == "Q" and k > 1:
                    stage_q(k - 1, QP if k < NSLOT - 1 else QP22)
            nd = 0
            sqs = []
            run("S", k - LSQ, sqs.append)
            pieces = [(j, i) for j in sqs for i in range(4)]
            for c in SORD:
                if c == "0":
                    if k > 0:
                        stage_d(k, nd, False)
                    nd += 1
                if c == "1":
                    for j, i in pieces[0:2]:
                        stage_sq(j, i)
                    pieces = pieces[2:]
                if c == "r":
                    run("r", k - LX, stage_rsqrt)
            for j, i in pieces:
                stage_sq(j, i)
            run("C", k - LC, do_c)
            if k in (1, 2) and not BIASDMA:
                bias_pair(2 * k + 2, BV)
                bias_pair(2 * k + 3, BV)
            if k >= 2:
                stage_m(k - 2, (1,) if SPLIT else (0, 1))

        nxt["M"] = NSLOT - 2
        last = NSLOT - 1
        stage_q(last, QPL)
        run("M", last, stage_m)

        def square_all(j):
            for i in range(4):
                stage_sq(j, i)

        for j in range(nxt["A"], NSLOT):
            run("A", j, do_a)
            run("S", j, square_all)
            run("X", j - GT, stage_max)
            run("r", j - GT, stage_rsqrt)
            run("C", j - GT, do_c)
